import numpy as np
import ml_dtypes


def mxq(x, axis, fmt="e4m3"):
    dtype, down = {"e4m3": (ml_dtypes.float8_e4m3fn, 7), "e5m2": (ml_dtypes.float8_e5m2, 14)}[fmt]
    v = np.moveaxis(np.asarray(x, np.float32).astype(ml_dtypes.bfloat16).astype(np.float64), axis, -1)
    blocks = v.reshape(v.shape[:-1] + (-1, 32))
    amax = np.abs(blocks).max(-1, keepdims=True)
    byte = np.maximum(np.where(amax > 0, np.frexp(amax)[1] - 1 + 127, 0) - down, 1)
    scale = np.exp2(byte - 127.0)
    codes = (blocks / scale).astype(np.float32).astype(dtype).astype(np.float64)
    return np.moveaxis((codes * scale).reshape(v.shape), -1, axis)


WIDE = False


def mx_kscale(k):
    if not WIDE:
        return np.ones(k)
    levels = np.array([20, -20, 10, -10, 0])
    a = np.random.permutation(np.resize(levels, k // 512 * 4)).reshape(k // 512, 4)
    idx = np.arange(k)
    return np.exp2(a[idx // 512, idx % 128 // 32])


BF16 = ml_dtypes.bfloat16


def bf(x):
    return np.asarray(x, np.float32).astype(BF16)


def f64(x):
    return np.asarray(x).astype(np.float64)


B, EN_MID, DE_MID = 512, 2048, 4096
K1 = EN_MID // 2
K2 = DE_MID // 2


def setup_inputs():
    s = mx_kscale(B)
    in0 = bf(np.random.standard_normal((B, K1, 2)).reshape(B, EN_MID))
    W = bf(np.random.standard_normal((DE_MID, K1)) / np.sqrt(K1))
    bias = bf(np.random.standard_normal(DE_MID) * 0.25)
    g = bf(np.random.standard_normal((B, DE_MID, 1)) * np.exp2(np.random.randint(-12, 1, (B, 1, 1))) / s[:, None, None])
    z = f64(in0).reshape(B, K1, 2)[:, :, 1] @ f64(W).T + f64(bias)
    return {"in_data": bf(f64(in0) * s[:, None]), "W": W, "bias": bias,
            "z": np.asarray(z, np.float32), "grad_out": g}


def reference(in_data, W, bias, z, grad_out):
    n = in_data.shape[0]
    x = f64(in_data).reshape(n, K1, 2)[:, :, 1]
    gr = f64(grad_out).reshape(n, K2, 2)[:, :, 0]
    dact = np.concatenate([gr, -gr], axis=1)
    dz = np.where(f64(z) > 0.0, dact, 0.0)
    return mxq(dz, 0, "e5m2").T @ mxq(x, 0, "e4m3")

@@ -1,0 +1,121 @@
+from contextlib import ExitStack
+
+import concourse.mybir as mybir
+
+F32 = mybir.dt.float32
+BF16 = mybir.dt.bfloat16
+U32 = mybir.dt.uint32
+U8 = mybir.dt.uint8
+E4M3_X4 = mybir.dt.float8_e4m3fn_x4
+E5M2_X4 = mybir.dt.float8_e5m2_x4
+ALU = mybir.AluOpType
+
+P = 128
+PACK = 4
+TOKENS = P * PACK
+X_COLS = 1024
+GR_COLS = 2048
+M_TILE = 128
+N_TILE = 512
+CHUNK = 512
+LOAD_COLS = 1024
+
+FLOPS = 2 * TOKENS * 2 * GR_COLS * X_COLS
+BYTES = TOKENS * X_COLS * 2 + TOKENS * GR_COLS * 2 + TOKENS * 2 * GR_COLS * 4 + 2 * GR_COLS * X_COLS * 4
+
+
+def tile_middlelayer_v_kernel(tc, in_data, W, bias, z, grad_out, out):
+    nc = tc.nc
+    groups = GR_COLS // LOAD_COLS
+
+    in_view = in_data.rearrange("(p t) c -> p t c", t=PACK)
+    g_view = grad_out.rearrange("(p t) c o -> p t (c o)", t=PACK)
+    z_view = z.rearrange("(p t) c -> p t c", t=PACK)
+
+    with ExitStack() as ctx:
+        x_pool = ctx.enter_context(tc.tile_pool(name="x", bufs=1))
+        g_pool = ctx.enter_context(tc.tile_pool(name="g", bufs=groups))
+        z_pool = ctx.enter_context(tc.tile_pool(name="z", bufs=2 * groups))
+        work = ctx.enter_context(tc.tile_pool(name="work", bufs=3))
+        out_pool = ctx.enter_context(tc.tile_pool(name="out", bufs=4))
+        psum = ctx.enter_context(tc.psum_pool(name="psum", bufs=8))
+
+        in_sb = x_pool.tile([P, PACK, 2 * X_COLS], BF16)
+        nc.sync.dma_start(out=in_sb[:], in_=in_view)
+        g_tiles = []
+        z_tiles = []
+        for grp in range(groups):
+            g_sb = g_pool.tile([P, PACK, 2 * LOAD_COLS], BF16)
+            nc.sync.dma_start(out=g_sb[:], in_=g_view[:, :, 2 * grp * LOAD_COLS : 2 * (grp + 1) * LOAD_COLS])
+            g_tiles.append(g_sb)
+            for half in range(2):
+                first = half * GR_COLS + grp * LOAD_COLS
+                z_sb = z_pool.tile([P, PACK, LOAD_COLS], F32)
+                nc.sync.dma_start(out=z_sb[:], in_=z_view[:, :, first : first + LOAD_COLS])
+                z_tiles.append(z_sb)
+
+        x_words = x_pool.tile([P, X_COLS, PACK], BF16, align_bytes=64)
+        imaginary = in_sb[:].rearrange("p t (k two) -> p t k two", two=2)[:, :, :, 1]
+        nc.vector.tensor_copy(out=x_words[:], in_=imaginary.rearrange("p t k -> p k t"))
+        x_codes = x_pool.tile([P, X_COLS], U32, align_bytes=64)
+        x_scales = x_pool.tile([P, X_COLS], U8, align_bytes=64)
+        nc.vector.quantize_mx(
+            out=x_codes[:].bitcast(E4M3_X4),
+            scales=x_scales[:],
+            in_=x_words[:].rearrange("p k t -> p (k t)"),
+        )
+
+        for grp in range(groups):
+            g_even = g_tiles[grp][:].rearrange("p t (w two) -> p t w two", two=2)[:, :, :, 0]
+            for half, sign in ((0, 1.0), (1, -1.0)):
+                z_sb = z_tiles[2 * grp + half]
+                for c in range(LOAD_COLS // CHUNK):
+                    cols = slice(c * CHUNK, (c + 1) * CHUNK)
+
+                    masked = work.tile([P, PACK, CHUNK], BF16)
+                    nc.vector.scalar_tensor_tensor(
+                        out=masked[:],
+                        in0=z_sb[:, :, cols],
+                        scalar=0.0,
+                        in1=g_even[:, :, cols],
+                        op0=ALU.is_gt,
+                        op1=ALU.mult,
+                    )
+                    dz_words = work.tile([P, CHUNK, PACK], BF16, align_bytes=64)
+                    nc.vector.tensor_scalar(
+                        out=dz_words[:].rearrange("p (c i) t -> p c t i", i=4),
+                        in0=masked[:].rearrange("p t (c i) -> p c t i", i=4),
+                        scalar1=sign,
+                        scalar2=None,
+                        op0=ALU.mult,
+                    )
+                    dz_codes = work.tile([P, CHUNK], U32, align_bytes=64)
+                    dz_scales = work.tile([P, CHUNK], U8, align_bytes=64)
+                    nc.vector.quantize_mx(
+                        out=dz_codes[:].bitcast(E5M2_X4),
+                        scales=dz_scales[:],
+                        in_=dz_words[:].rearrange("p w t -> p (w t)"),
+                    )
+
+                    result = out_pool.tile([P, CHUNK // M_TILE, X_COLS], F32)
+                    for m in range(CHUNK // M_TILE):
+                        m_cols = slice(m * M_TILE, (m + 1) * M_TILE)
+                        for n in range(X_COLS // N_TILE):
+                            n_cols = slice(n * N_TILE, (n + 1) * N_TILE)
+                            acc = psum.tile([M_TILE, N_TILE], F32)
+                            nc.tensor.matmul_mx(
+                                out=acc[:],
+                                lhsT=dz_codes[:, m_cols].bitcast(E5M2_X4),
+                                lhsT_scale=dz_scales[:, m_cols],
+                                rhs=x_codes[:, n_cols].bitcast(E4M3_X4),
+                                rhs_scale=x_scales[:, n_cols],
+                                start=True,
+                                stop=True,
+                            )
+                            nc.scalar.copy(out=result[:, m, n_cols], in_=acc[:])
+
+                    first_row = half * GR_COLS + grp * LOAD_COLS + c * CHUNK
+                    nc.sync.dma_start(
+                        out=out[first_row : first_row + CHUNK, :].rearrange("(m q) n -> q m n", q=M_TILE),
+                        in_=result[:],
+                    )

@@ -18,6 +18,7 @@ GR_COLS = 2048
 M_TILE = 128
 N_TILE = 512
 CHUNK = 512
+M_TILES = CHUNK // M_TILE
 LOAD_COLS = 1024
 
 FLOPS = 2 * TOKENS * 2 * GR_COLS * X_COLS
@@ -81,10 +82,10 @@ def tile_middlelayer_v_kernel(tc, in_data, W, bias, z, grad_out, out):
                         op0=ALU.is_gt,
                         op1=ALU.mult,
                     )
-                    dz_words = work.tile([P, CHUNK, PACK], BF16, align_bytes=64)
+                    dz_words = work.tile([P, M_TILES, M_TILE, PACK], BF16, align_bytes=64)
                     nc.vector.tensor_scalar(
-                        out=dz_words[:].rearrange("p (c i) t -> p c t i", i=4),
-                        in0=masked[:].rearrange("p t (c i) -> p c t i", i=4),
+                        out=dz_words[:].rearrange("p m q t -> p q t m"),
+                        in0=masked[:].rearrange("p t (q m) -> p q t m", m=M_TILES),
                         scalar1=sign,
                         scalar2=None,
                         op0=ALU.mult,
@@ -94,11 +95,11 @@ def tile_middlelayer_v_kernel(tc, in_data, W, bias, z, grad_out, out):
                     nc.vector.quantize_mx(
                         out=dz_codes[:].bitcast(E5M2_X4),
                         scales=dz_scales[:],
-                        in_=dz_words[:].rearrange("p w t -> p (w t)"),
+                        in_=dz_words[:].rearrange("p m q t -> p (m q t)"),
                     )
 
-                    result = out_pool.tile([P, CHUNK // M_TILE, X_COLS], F32)
-                    for m in range(CHUNK // M_TILE):
+                    result = out_pool.tile([P, M_TILES, X_COLS], F32)
+                    for m in range(M_TILES):
                         m_cols = slice(m * M_TILE, (m + 1) * M_TILE)
                         for n in range(X_COLS // N_TILE):
                             n_cols = slice(n * N_TILE, (n + 1) * N_TILE)
@@ -116,6 +117,6 @@ def tile_middlelayer_v_kernel(tc, in_data, W, bias, z, grad_out, out):
 
                     first_row = half * GR_COLS + grp * LOAD_COLS + c * CHUNK
                     nc.sync.dma_start(
-                        out=out[first_row : first_row + CHUNK, :].rearrange("(m q) n -> q m n", q=M_TILE),
+                        out=out[first_row : first_row + CHUNK, :].rearrange("(q m) n -> q m n", m=M_TILES),
                         in_=result[:],
                     )

@@ -41,17 +41,17 @@ def tile_middlelayer_v_kernel(tc, in_data, W, bias, z, grad_out, out):
         out_pool = ctx.enter_context(tc.tile_pool(name="out", bufs=4))
         psum = ctx.enter_context(tc.psum_pool(name="psum", bufs=8))
 
-        in_sb = x_pool.tile([P, PACK, 2 * X_COLS], BF16)
+        in_sb = x_pool.tile([P, PACK, 2 * X_COLS], BF16, align_bytes=256)
         nc.sync.dma_start(out=in_sb[:], in_=in_view)
         g_tiles = []
         z_tiles = []
         for grp in range(groups):
-            g_sb = g_pool.tile([P, PACK, 2 * LOAD_COLS], BF16)
+            g_sb = g_pool.tile([P, PACK, 2 * LOAD_COLS], BF16, align_bytes=256)
             nc.sync.dma_start(out=g_sb[:], in_=g_view[:, :, 2 * grp * LOAD_COLS : 2 * (grp + 1) * LOAD_COLS])
             g_tiles.append(g_sb)
             for half in range(2):
                 first = half * GR_COLS + grp * LOAD_COLS
-                z_sb = z_pool.tile([P, PACK, LOAD_COLS], F32)
+                z_sb = z_pool.tile([P, PACK, LOAD_COLS], F32, align_bytes=256)
                 nc.sync.dma_start(out=z_sb[:], in_=z_view[:, :, first : first + LOAD_COLS])
                 z_tiles.append(z_sb)
 
@@ -98,7 +98,7 @@ def tile_middlelayer_v_kernel(tc, in_data, W, bias, z, grad_out, out):
                         in_=dz_words[:].rearrange("p m q t -> p (m q t)"),
                     )
 
-                    result = out_pool.tile([P, M_TILES, X_COLS], F32)
+                    result = out_pool.tile([P, M_TILES, X_COLS], F32, align_bytes=256)
                     for m in range(M_TILES):
                         m_cols = slice(m * M_TILE, (m + 1) * M_TILE)
                         for n in range(X_COLS // N_TILE):

@@ -41,17 +41,17 @@ def tile_middlelayer_v_kernel(tc, in_data, W, bias, z, grad_out, out):
         out_pool = ctx.enter_context(tc.tile_pool(name="out", bufs=4))
         psum = ctx.enter_context(tc.psum_pool(name="psum", bufs=8))
 
-        in_sb = x_pool.tile([P, PACK, 2 * X_COLS], BF16, align_bytes=256)
+        in_sb = x_pool.tile([P, PACK, 2 * X_COLS], BF16, align_bytes=4096)
         nc.sync.dma_start(out=in_sb[:], in_=in_view)
         g_tiles = []
         z_tiles = []
         for grp in range(groups):
-            g_sb = g_pool.tile([P, PACK, 2 * LOAD_COLS], BF16, align_bytes=256)
+            g_sb = g_pool.tile([P, PACK, 2 * LOAD_COLS], BF16, align_bytes=4096)
             nc.sync.dma_start(out=g_sb[:], in_=g_view[:, :, 2 * grp * LOAD_COLS : 2 * (grp + 1) * LOAD_COLS])
             g_tiles.append(g_sb)
             for half in range(2):
                 first = half * GR_COLS + grp * LOAD_COLS
-                z_sb = z_pool.tile([P, PACK, LOAD_COLS], F32, align_bytes=256)
+                z_sb = z_pool.tile([P, PACK, LOAD_COLS], F32, align_bytes=4096)
                 nc.sync.dma_start(out=z_sb[:], in_=z_view[:, :, first : first + LOAD_COLS])
                 z_tiles.append(z_sb)
 
@@ -98,7 +98,7 @@ def tile_middlelayer_v_kernel(tc, in_data, W, bias, z, grad_out, out):
                         in_=dz_words[:].rearrange("p m q t -> p (m q t)"),
                     )
 
-                    result = out_pool.tile([P, M_TILES, X_COLS], F32, align_bytes=256)
+                    result = out_pool.tile([P, M_TILES, X_COLS], F32, align_bytes=4096)
                     for m in range(M_TILES):
                         m_cols = slice(m * M_TILE, (m + 1) * M_TILE)
                         for n in range(X_COLS // N_TILE):

from contextlib import ExitStack

import concourse.mybir as mybir

F32 = mybir.dt.float32
BF16 = mybir.dt.bfloat16
U32 = mybir.dt.uint32
U8 = mybir.dt.uint8
E4M3_X4 = mybir.dt.float8_e4m3fn_x4
E5M2_X4 = mybir.dt.float8_e5m2_x4
ALU = mybir.AluOpType

P = 128
PACK = 4
TOKENS = P * PACK
X_COLS = 1024
GR_COLS = 2048
M_TILE = 128
N_TILE = 512
CHUNK = 512
M_TILES = CHUNK // M_TILE
LOAD_COLS = 1024

FLOPS = 2 * TOKENS * 2 * GR_COLS * X_COLS
BYTES = TOKENS * X_COLS * 2 + TOKENS * GR_COLS * 2 + TOKENS * 2 * GR_COLS * 4 + 2 * GR_COLS * X_COLS * 4


def tile_middlelayer_v_kernel(tc, in_data, W, bias, z, grad_out, out):
    nc = tc.nc
    groups = GR_COLS // LOAD_COLS

    in_view = in_data.rearrange("(p t) c -> p t c", t=PACK)
    g_view = grad_out.rearrange("(p t) c o -> p t (c o)", t=PACK)
    z_view = z.rearrange("(p t) c -> p t c", t=PACK)

    with ExitStack() as ctx:
        x_pool = ctx.enter_context(tc.tile_pool(name="x", bufs=1))
        g_pool = ctx.enter_context(tc.tile_pool(name="g", bufs=groups))
        z_pool = ctx.enter_context(tc.tile_pool(name="z", bufs=2 * groups))
        work = ctx.enter_context(tc.tile_pool(name="work", bufs=3))
        out_pool = ctx.enter_context(tc.tile_pool(name="out", bufs=4))
        psum = ctx.enter_context(tc.psum_pool(name="psum", bufs=8))

        in_sb = x_pool.tile([P, PACK, 2 * X_COLS], BF16, align_bytes=4096)
        nc.sync.dma_start(out=in_sb[:], in_=in_view)
        g_tiles = []
        z_tiles = []
        for grp in range(groups):
            g_sb = g_pool.tile([P, PACK, 2 * LOAD_COLS], BF16, align_bytes=4096)
            nc.sync.dma_start(out=g_sb[:], in_=g_view[:, :, 2 * grp * LOAD_COLS : 2 * (grp + 1) * LOAD_COLS])
            g_tiles.append(g_sb)
            for half in range(2):
                first = half * GR_COLS + grp * LOAD_COLS
                z_sb = z_pool.tile([P, PACK, LOAD_COLS], F32, align_bytes=4096)
                nc.sync.dma_start(out=z_sb[:], in_=z_view[:, :, first : first + LOAD_COLS])
                z_tiles.append(z_sb)

        x_words = x_pool.tile([P, X_COLS, PACK], BF16, align_bytes=64)
        imaginary = in_sb[:].rearrange("p t (k two) -> p t k two", two=2)[:, :, :, 1]
        nc.vector.tensor_copy(out=x_words[:], in_=imaginary.rearrange("p t k -> p k t"))
        x_codes = x_pool.tile([P, X_COLS], U32, align_bytes=64)
        x_scales = x_pool.tile([P, X_COLS], U8, align_bytes=64)
        nc.vector.quantize_mx(
            out=x_codes[:].bitcast(E4M3_X4),
            scales=x_scales[:],
            in_=x_words[:].rearrange("p k t -> p (k t)"),
        )

        for grp in range(groups):
            g_even = g_tiles[grp][:].rearrange("p t (w two) -> p t w two", two=2)[:, :, :, 0]
            for half, sign in ((0, 1.0), (1, -1.0)):
                z_sb = z_tiles[2 * grp + half]
                for c in range(LOAD_COLS // CHUNK):
                    cols = slice(c * CHUNK, (c + 1) * CHUNK)

                    masked = work.tile([P, PACK, CHUNK], BF16)
                    nc.vector.scalar_tensor_tensor(
                        out=masked[:],
                        in0=z_sb[:, :, cols],
                        scalar=0.0,
                        in1=g_even[:, :, cols],
                        op0=ALU.is_gt,
                        op1=ALU.mult,
                    )
                    dz_words = work.tile([P, M_TILES, M_TILE, PACK], BF16, align_bytes=64)
                    nc.vector.tensor_scalar(
                        out=dz_words[:].rearrange("p m q t -> p q t m"),
                        in0=masked[:].rearrange("p t (q m) -> p q t m", m=M_TILES),
                        scalar1=sign,
                        scalar2=None,
                        op0=ALU.mult,
                    )
                    dz_codes = work.tile([P, CHUNK], U32, align_bytes=64)
                    dz_scales = work.tile([P, CHUNK], U8, align_bytes=64)
                    nc.vector.quantize_mx(
                        out=dz_codes[:].bitcast(E5M2_X4),
                        scales=dz_scales[:],
                        in_=dz_words[:].rearrange("p m q t -> p (m q t)"),
                    )

                    result = out_pool.tile([P, M_TILES, X_COLS], F32, align_bytes=4096)
                    for m in range(M_TILES):
                        m_cols = slice(m * M_TILE, (m + 1) * M_TILE)
                        for n in range(X_COLS // N_TILE):
                            n_cols = slice(n * N_TILE, (n + 1) * N_TILE)
                            acc = psum.tile([M_TILE, N_TILE], F32)
                            nc.tensor.matmul_mx(
                                out=acc[:],
                                lhsT=dz_codes[:, m_cols].bitcast(E5M2_X4),
                                lhsT_scale=dz_scales[:, m_cols],
                                rhs=x_codes[:, n_cols].bitcast(E4M3_X4),
                                rhs_scale=x_scales[:, n_cols],
                                start=True,
                                stop=True,
                            )
                            nc.scalar.copy(out=result[:, m, n_cols], in_=acc[:])

                    first_row = half * GR_COLS + grp * LOAD_COLS + c * CHUNK
                    nc.sync.dma_start(
                        out=out[first_row : first_row + CHUNK, :].rearrange("(q m) n -> q m n", m=M_TILES),
                        in_=result[:],
                    )
